import numpy as np
import ml_dtypes


BF16 = ml_dtypes.bfloat16


def bf(x):
    return np.asarray(x, np.float32).astype(BF16)


def f64(x):
    return np.asarray(x).astype(np.float64)


E2M1 = np.array([0.0, 0.5, 1.0, 1.5, 2.0, 3.0, 4.0, 6.0, -0.0, -0.5, -1.0, -1.5, -2.0, -3.0, -4.0, -6.0])


def pack_weight(w, fmt):
    k, n = w.shape
    w = f64(bf(w)).reshape(k // 32, 32, n)
    amax = np.abs(w).max(1)
    if fmt == "e4m3":
        byte = np.frexp(amax)[1] - 1 + 127 - 7
    else:
        mant, ex = np.frexp(amax / 6.0)
        byte = np.where(mant > 0.5, ex, ex - 1) + 127
    byte = np.clip(np.where(amax > 0, byte, 1), 1, 254)
    scaled = (w * np.exp2(127.0 - byte)[:, None, :]).reshape(k, n).astype(np.float32)
    by_word = np.ascontiguousarray(scaled.reshape(k // 512, 128, 4, n).transpose(0, 1, 3, 2))
    if fmt == "e4m3":
        words = by_word.astype(ml_dtypes.float8_e4m3fn).view(np.uint8)
    else:
        c = by_word.astype(ml_dtypes.float4_e2m1fn).view(np.uint8) & 0xF
        words = c[..., 0::2] | (c[..., 1::2] << 4)
    return np.ascontiguousarray(words), np.ascontiguousarray(byte.astype(np.uint8).reshape(k // 512, 16, n))


def unpack_weight(words, scales, fmt):
    g, p, n, _ = words.shape
    if fmt == "e4m3":
        vals = np.ascontiguousarray(words).view(ml_dtypes.float8_e4m3fn).astype(np.float64)
    else:
        nib = np.empty((g, p, n, 4), np.uint8)
        nib[..., 0::2] = words & 0xF
        nib[..., 1::2] = words >> 4
        vals = E2M1[nib]
    vals = vals * np.repeat(np.exp2(scales.astype(np.float64) - 127.0), 8, axis=1)[..., None]
    return vals.transpose(0, 1, 3, 2).reshape(g * 512, n)

def pack4(w):
    words, scales = pack_weight(w, "e2m1")
    return words.reshape(words.shape[0], 128, -1), scales


def unpack4(words, scales):
    return unpack_weight(words.reshape(words.shape[0], 128, -1, 2), scales, "e2m1")


def kspread(k):
    return np.exp2(np.repeat(np.random.randint(-6, 7, k // 32), 32).astype(np.float64))


B, S, H, D = 2, 64, 4, 2560

EPS = 2.0 ** -23


def rms_normalize(v):
    ms = np.mean(v * v, axis=-1, keepdims=True)
    return v / np.sqrt(ms + EPS)


def sigmoid(v):
    return 1.0 / (1.0 + np.exp(-v))


def setup_inputs():
    s = kspread(D)
    embeddings = np.random.standard_normal((B, S, D)) * s
    embeddings_words, embeddings_scales = pack4(embeddings.reshape(B * S, D).T)
    hidden_states = bf(np.random.standard_normal((B, S, H, D)))
    wv = np.random.standard_normal((D, D)) / np.sqrt(D) / s
    Wv_words, Wv_scales = pack4(wv.T)
    bv = bf(np.random.standard_normal(D) * 0.5)
    wk = np.random.standard_normal((H, D, D)) / np.sqrt(D) / s
    Wk_words, Wk_scales = pack4(wk.reshape(H * D, D).T)
    return {"embeddings_words": embeddings_words,
            "embeddings_scales": embeddings_scales,
            "hidden_states": hidden_states,
            "Wv_words": Wv_words,
            "Wv_scales": Wv_scales,
            "bv": bv,
            "Wk_words": Wk_words,
            "Wk_scales": Wk_scales,
            "bk": bf(np.random.standard_normal((H, D)) * 0.5),
            "g1": bf(1.0 + 0.3 * np.random.standard_normal((H, D))),
            "g2": bf(1.0 + 0.3 * np.random.standard_normal((H, D)))}


def reference(embeddings_words, embeddings_scales, hidden_states, Wv_words, Wv_scales, bv, Wk_words, Wk_scales, bk, g1, g2):
    eq = unpack4(embeddings_words, embeddings_scales).T.reshape(B, S, D)
    wkq = unpack4(Wk_words, Wk_scales).T.reshape(H, D, D)
    key = (eq @ wkq.reshape(H * D, D).T).reshape(B, S, H, D) + f64(bk)
    normed_key = rms_normalize(key) * f64(g1)
    normed_query = rms_normalize(f64(hidden_states)) * f64(g2)
    gate = np.sum(normed_key * normed_query, axis=-1) / np.sqrt(D)
    gate = np.sqrt(np.maximum(np.abs(gate), 1e-6)) * np.sign(gate)
    gate = sigmoid(gate)[..., None]
    value = ((eq @ unpack4(Wv_words, Wv_scales)) + f64(bv))[:, :, None, :]
    return gate * value

@@ -1,0 +1,287 @@
+from contextlib import ExitStack
+
+import concourse.mybir as mybir
+from concourse.masks import make_identity
+
+FLOPS = 2 * 128 * 2560 * 12800
+
+F32 = mybir.dt.float32
+BF16 = mybir.dt.bfloat16
+U8 = mybir.dt.uint8
+I32 = mybir.dt.int32
+FP4X4 = mybir.dt.float4_e2m1fn_x4
+ALU = mybir.AluOpType
+FN = mybir.ActivationFunctionType
+AX = mybir.AxisListType
+
+P = 128
+D = 2560
+H = 4
+PASSES = 5
+NT = 512
+CH = D // NT
+EPS = 2.0 ** -23
+HALF = D // 2
+HALF_GROUPS = ((0, 512), (512, 512), (1024, 256))
+N_PLANES = 3
+
+
+def tile_engramgating_kernel(
+    tc,
+    embeddings_words,
+    embeddings_scales,
+    hidden_states,
+    Wv_words,
+    Wv_scales,
+    bv,
+    Wk_words,
+    Wk_scales,
+    bk,
+    g1,
+    g2,
+    out,
+):
+    nc = tc.nc
+    hs_view = hidden_states.rearrange("b s h d -> (b s) h d")
+    out_view = out.rearrange("b s h d -> (b s) h d")
+
+    with ExitStack() as ctx:
+        keep = ctx.enter_context(tc.tile_pool(name="keep", bufs=1))
+        codes = ctx.enter_context(tc.tile_pool(name="codes", bufs=12))
+        big = ctx.enter_context(tc.tile_pool(name="big", bufs=4))
+        work = ctx.enter_context(tc.tile_pool(name="work", bufs=2))
+        ps = ctx.enter_context(tc.psum_pool(name="ps", bufs=8))
+        ctx.enter_context(tc.manual_schedule())
+
+        ident = keep.tile([P, P], BF16, name="ident")
+        selg = keep.tile([P, 32], BF16, name="selg")
+        g1t = keep.tile([64, NT], BF16, name="g1t")
+        g2t = keep.tile([64, NT], BF16, name="g2t")
+        gprod = keep.tile([64, NT], F32, name="gprod")
+        ghi = keep.tile([64, NT], BF16, name="ghi")
+        rows = keep.tile([P, NT], BF16, name="rows")
+        embc = keep.tile([P, PASSES, 2 * P], U8, name="embc", align_bytes=64)
+        embp = keep.tile([P, PASSES, P], U8, name="embp", align_bytes=64)
+        planes = []
+        for i in range(N_PLANES):
+            pl = keep.tile([P, PASSES, D], U8, name="plane%d" % i, align_bytes=64)
+            planes.append(pl)
+        bvb = keep.tile([P, D], BF16, name="bvb")
+        vb = keep.tile([P, D], F32, name="vb")
+        st5 = keep.tile([P, 3, H, CH], F32, name="st5")
+        st = keep.tile([P, 3, H], F32, name="st")
+        msq = keep.tile([P, 2, H], F32, name="msq")
+        rms = keep.tile([P, 2, H], F32, name="rms")
+        den = keep.tile([P, H], F32, name="den")
+        rden = keep.tile([P, H], F32, name="rden")
+        aval = keep.tile([P, H], F32, name="aval")
+        aabs = keep.tile([P, H], F32, name="aabs")
+        aclip = keep.tile([P, H], F32, name="aclip")
+        aroot = keep.tile([P, H], F32, name="aroot")
+        asign = keep.tile([P, H], F32, name="asign")
+        cval = keep.tile([P, H], F32, name="cval")
+        gate = keep.tile([P, H], F32, name="gate")
+        one = keep.tile([P, 1], F32, name="one")
+        warm = keep.tile([P, 1], F32, name="warm")
+
+        def load_scales(plane, scales_dram, c0, width):
+            for r in range(4):
+                nc.sync.dma_start(
+                    out=plane[r:P:32, :, 0:width].bitcast(I32),
+                    in_=scales_dram[:, r:16:4, c0 : c0 + width].rearrange("g q n -> q g n").bitcast(I32),
+                )
+
+        def load_codes(words_dram, g, c0, width):
+            ct = codes.tile([P, 2 * width], U8, name="ct", tag="ct", align_bytes=64)
+            nc.sync.dma_start(
+                out=ct[:].bitcast(I32),
+                in_=words_dram[g, :, 2 * c0 : 2 * (c0 + width)].bitcast(I32),
+            )
+            return ct
+
+        def mx(acc, g, ct, off, plane, col, n):
+            nc.tensor.matmul_mx(
+                out=acc[:, 0:n],
+                lhsT=embc[:, g, :].bitcast(FP4X4),
+                lhsT_scale=embp[:, g, :],
+                rhs=ct[:, 2 * off : 2 * (off + n)].bitcast(FP4X4),
+                rhs_scale=plane[:, g, col : col + n],
+                start=(g == 0),
+                stop=(g == PASSES - 1),
+            )
+
+        nc.vector.memset(g1t[:], 0.0)
+        nc.vector.memset(g2t[:], 0.0)
+        nc.vector.memset(rows[:], 0.0)
+        nc.vector.memset(one[:], 1.0)
+        nc.vector.memset(embp[:].bitcast(I32), 0)
+        nc.vector.memset(planes[0][:].bitcast(I32), 0)
+        make_identity(nc, ident[:])
+        nc.gpsimd.memset(planes[1][:].bitcast(F32), 0.0)
+        nc.gpsimd.memset(planes[2][:].bitcast(F32), 0.0)
+
+        g1v = g1.rearrange("h (c n) -> (h c) n", n=NT)
+        g2v = g2.rearrange("h (c n) -> (h c) n", n=NT)
+        bkv = bk.rearrange("h (c n) -> (h c) n", n=NT)
+        bvv = bv.rearrange("(c n) -> c n", n=NT)
+        nc.scalar.dma_start(out=g1t[0 : H * CH, :], in_=g1v)
+        nc.scalar.dma_start(out=g2t[0 : H * CH, :], in_=g2v)
+        nc.scalar.dma_start(out=g1t[32 : 32 + H * CH, :], in_=g1v)
+        nc.scalar.dma_start(out=g2t[32 : 32 + H * CH, :], in_=g2v)
+        nc.scalar.dma_start(out=rows[64 : 64 + H * CH, :], in_=bkv)
+        nc.scalar.dma_start(out=rows[96 : 96 + CH, :], in_=bvv)
+        nc.scalar.activation(out=warm[:], in_=one[:], func=FN.Sqrt)
+
+        nc.sync.dma_start(
+            out=embc[:].bitcast(I32),
+            in_=embeddings_words.rearrange("g p n -> p g n").bitcast(I32),
+        )
+        hs = []
+        for h in range(H):
+            hst = big.tile([P, D], BF16, name="hst", tag="hs")
+            nc.sync.dma_start(out=hst[:], in_=hs_view[:, h, :])
+            hs.append(hst)
+        load_scales(embp, embeddings_scales, 0, P)
+
+        def load_unit(u):
+            plane = planes[u % N_PLANES]
+            if u < H:
+                load_scales(plane, Wk_scales, u * D, D)
+                return [[load_codes(Wk_words, g, u * D, D) for g in range(PASSES)]]
+            load_scales(plane, Wv_scales, 0, D)
+            return [[load_codes(Wv_words, g, half * HALF, HALF) for g in range(PASSES)] for half in range(2)]
+
+        loaded = {0: load_unit(0)}
+
+        nc.vector.tensor_tensor(out=gprod[:], in0=g1t[:], in1=g2t[:], op=ALU.mult)
+        nc.vector.tensor_tensor(out=selg[:], in0=ident[:, 0:32], in1=ident[:, 32:64], op=ALU.add)
+        nc.vector.tensor_copy(out=rows[0:32, :], in_=gprod[0:32, :])
+        nc.vector.tensor_copy(out=ghi[32:64, :], in_=gprod[32:64, :])
+        nc.vector.tensor_tensor(out=rows[32:64, :], in0=gprod[32:64, :], in1=ghi[32:64, :], op=ALU.subtract)
+
+        def spread(sel_col):
+            pt = ps.tile([P, NT], F32, name="pt", tag="ps")
+            nc.tensor.matmul(out=pt[:], lhsT=sel_col.to_broadcast([P, P]), rhs=rows[:], start=True, stop=True)
+            return pt
+
+        wts = []
+        bkbs = []
+        for h in range(H):
+            wt = big.tile([P, D], F32, name="wt", tag="w")
+            bkb = big.tile([P, D], BF16, name="bkb", tag="bkb")
+            wts.append(wt)
+            bkbs.append(bkb)
+            for j in range(CH):
+                c = h * CH + j
+                cs = slice(j * NT, (j + 1) * NT)
+                pg = spread(selg[:, c : c + 1])
+                pb = spread(ident[:, 64 + c : 65 + c])
+                nc.vector.tensor_tensor(out=wt[:, cs], in0=pg[:], in1=hs[h][:, cs], op=ALU.mult)
+                nc.scalar.copy(out=bkb[:, cs], in_=pb[:])
+        for j in range(CH):
+            cs = slice(j * NT, (j + 1) * NT)
+            pb = spread(ident[:, 96 + j : 97 + j])
+            nc.scalar.copy(out=bvb[:, cs], in_=pb[:])
+
+        def chain1(a, b):
+            nc.vector.tensor_reduce(out=st[:, :, a:b], in_=st5[:, :, a:b, :], axis=AX.X, op=ALU.add)
+            nc.vector.tensor_scalar(
+                out=msq[:, :, a:b], in0=st[:, 0:2, a:b], scalar1=1.0 / D, scalar2=EPS, op0=ALU.mult, op1=ALU.add
+            )
+            nc.scalar.activation(out=rms[:, :, a:b], in_=msq[:, :, a:b], func=FN.Sqrt)
+
+        def chain2(a, b):
+            nc.vector.tensor_tensor(out=den[:, a:b], in0=rms[:, 0, a:b], in1=rms[:, 1, a:b], op=ALU.mult)
+            nc.vector.reciprocal(out=rden[:, a:b], in_=den[:, a:b])
+            nc.vector.scalar_tensor_tensor(
+                out=aval[:, a:b], in0=st[:, 2, a:b], scalar=D ** -0.5, in1=rden[:, a:b], op0=ALU.mult, op1=ALU.mult
+            )
+            nc.vector.scalar_tensor_tensor(
+                out=aabs[:, a:b], in0=aval[:, a:b], scalar=-1.0, in1=aval[:, a:b], op0=ALU.mult, op1=ALU.max
+            )
+            nc.vector.tensor_scalar_max(out=aclip[:, a:b], in0=aabs[:, a:b], scalar1=1e-6)
+            nc.scalar.activation(out=aroot[:, a:b], in_=aclip[:, a:b], func=FN.Sqrt)
+            nc.scalar.activation(out=asign[:, a:b], in_=aval[:, a:b], func=FN.Sign)
+
+        def chain3(a, b):
+            nc.vector.tensor_tensor(out=cval[:, a:b], in0=aroot[:, a:b], in1=asign[:, a:b], op=ALU.mult)
+            nc.scalar.activation(out=gate[:, a:b], in_=cval[:, a:b], func=FN.Sigmoid)
+
+        for u in range(H):
+            loaded[u + 1] = load_unit(u + 1)
+            cts = loaded[u][0]
+            plane = planes[u % N_PLANES]
+            for j in range(CH):
+                cs = slice(j * NT, (j + 1) * NT)
+                js = work.tile([P, NT], BF16, name="js", tag="js")
+                nc.scalar.activation(
+                    out=js[:], in_=hs[u][:, cs], func=FN.Square, accum_out=st5[:, 1, u, j : j + 1]
+                )
+            accs = []
+            for j in range(CH):
+                acc = ps.tile([P, NT], F32, name="acc", tag="ps")
+                accs.append(acc)
+            for g in range(PASSES):
+                for j in range(CH):
+                    mx(accs[j], g, cts[g], j * NT, plane, j * NT, NT)
+            kbs = []
+            for j in range(CH):
+                cs = slice(j * NT, (j + 1) * NT)
+                kb = work.tile([P, NT], F32, name="kb", tag="kb", bufs=6)
+                kbs.append(kb)
+                nc.vector.tensor_tensor(out=kb[:], in0=accs[j][:], in1=bkbs[u][:, cs], op=ALU.add)
+                js = work.tile([P, NT], BF16, name="js", tag="js")
+                nc.scalar.activation(out=js[:], in_=kb[:], func=FN.Square, accum_out=st5[:, 0, u, j : j + 1])
+            for j in range(CH):
+                cs = slice(j * NT, (j + 1) * NT)
+                jv = work.tile([P, NT], F32, name="jv", tag="jv")
+                nc.vector.scalar_tensor_tensor(
+                    out=jv[:],
+                    in0=kbs[j][:],
+                    scalar=1.0,
+                    in1=wts[u][:, cs],
+                    op0=ALU.mult,
+                    op1=ALU.mult,
+                    accum_out=st5[:, 2, u, j : j + 1],
+                )
+            if u == H - 2:
+                chain1(0, H - 1)
+                chain2(0, H - 1)
+                chain3(0, H - 1)
+
+        chain1(H - 1, H)
+        plane = planes[H % N_PLANES]
+        outs = []
+        for h in range(H):
+            ot = big.tile([P, D], F32, name="ot", tag="w")
+            outs.append(ot)
+        for half in range(2):
+            cts = loaded[H][half]
+            c0 = half * HALF
+            hcs = slice(c0, c0 + HALF)
+            accs = []
+            for i in range(len(HALF_GROUPS)):
+                acc = ps.tile([P, NT], F32, name="acc", tag="ps")
+                accs.append(acc)
+            for g in range(PASSES):
+                for i, (off, n) in enumerate(HALF_GROUPS):
+                    mx(accs[i], g, cts[g], off, plane, c0 + off, n)
+            for i, (off, n) in enumerate(HALF_GROUPS):
+                cs = slice(c0 + off, c0 + off + n)
+                nc.vector.tensor_tensor(out=vb[:, cs], in0=accs[i][:, 0:n], in1=bvb[:, cs], op=ALU.add)
+            nc.vector.tensor_scalar_mul(out=outs[0][:, hcs], in0=vb[:, hcs], scalar1=gate[:, 0:1])
+            nc.scalar.activation(out=outs[1][:, hcs], in_=vb[:, hcs], func=FN.Copy, scale=gate[:, 1:2])
+            nc.vector.tensor_scalar_mul(out=outs[2][:, hcs], in0=vb[:, hcs], scalar1=gate[:, 2:3])
+            for h in range(H - 1):
+                nc.sync.dma_start(out=out_view[:, h, hcs], in_=outs[h][:, hcs])
+            if half == 0:
+                chain2(H - 1, H)
+            else:
+                chain3(H - 1, H)
+        last = H - 1
+        nc.vector.tensor_scalar_mul(out=outs[last][:, 0:HALF], in0=vb[:, 0:HALF], scalar1=gate[:, last : last + 1])
+        nc.scalar.activation(
+            out=outs[last][:, HALF:D], in_=vb[:, HALF:D], func=FN.Copy, scale=gate[:, last : last + 1]
+        )
+        nc.sync.dma_start(out=out_view[:, last, 0:HALF], in_=outs[last][:, 0:HALF])
+        nc.sync.dma_start(out=out_view[:, last, HALF:D], in_=outs[last][:, HALF:D])

@@ -23,7 +23,6 @@ CH = D // NT
 EPS = 2.0 ** -23
 HALF = D // 2
 HALF_GROUPS = ((0, 512), (512, 512), (1024, 256))
-N_PLANES = 3
 
 
 def tile_engramgating_kernel(
@@ -62,10 +61,11 @@ def tile_engramgating_kernel(
         rows = keep.tile([P, NT], BF16, name="rows")
         embc = keep.tile([P, PASSES, 2 * P], U8, name="embc", align_bytes=64)
         embp = keep.tile([P, PASSES, P], U8, name="embp", align_bytes=64)
-        planes = []
-        for i in range(N_PLANES):
-            pl = keep.tile([P, PASSES, D], U8, name="plane%d" % i, align_bytes=64)
-            planes.append(pl)
+        kplanes = []
+        for g in range(PASSES):
+            pl = keep.tile([P, H * D], U8, name="kplane%d" % g, align_bytes=64)
+            kplanes.append(pl)
+        vplane = keep.tile([P, PASSES, D], U8, name="vplane", align_bytes=64)
         bvb = keep.tile([P, D], BF16, name="bvb")
         vb = keep.tile([P, D], F32, name="vb")
         st5 = keep.tile([P, 3, H, CH], F32, name="st5")
@@ -99,13 +99,13 @@ def tile_engramgating_kernel(
             )
             return ct
 
-        def mx(acc, g, ct, off, plane, col, n):
+        def mx(acc, g, ct, off, scale_cols, n):
             nc.tensor.matmul_mx(
                 out=acc[:, 0:n],
                 lhsT=embc[:, g, :].bitcast(FP4X4),
                 lhsT_scale=embp[:, g, :],
                 rhs=ct[:, 2 * off : 2 * (off + n)].bitcast(FP4X4),
-                rhs_scale=plane[:, g, col : col + n],
+                rhs_scale=scale_cols,
                 start=(g == 0),
                 stop=(g == PASSES - 1),
             )
@@ -115,10 +115,12 @@ def tile_engramgating_kernel(
         nc.vector.memset(rows[:], 0.0)
         nc.vector.memset(one[:], 1.0)
         nc.vector.memset(embp[:].bitcast(I32), 0)
-        nc.vector.memset(planes[0][:].bitcast(I32), 0)
+        nc.vector.memset(kplanes[0][:].bitcast(I32), 0)
+        nc.vector.memset(kplanes[1][:].bitcast(I32), 0)
         make_identity(nc, ident[:])
-        nc.gpsimd.memset(planes[1][:].bitcast(F32), 0.0)
-        nc.gpsimd.memset(planes[2][:].bitcast(F32), 0.0)
+        for g in range(2, PASSES):
+            nc.gpsimd.memset(kplanes[g][:].bitcast(F32), 0.0)
+        nc.gpsimd.memset(vplane[:].bitcast(F32), 0.0)
 
         g1v = g1.rearrange("h (c n) -> (h c) n", n=NT)
         g2v = g2.rearrange("h (c n) -> (h c) n", n=NT)
@@ -138,17 +140,21 @@ def tile_engramgating_kernel(
         )
         hs = []
         for h in range(H):
-            hst = big.tile([P, D], BF16, name="hst", tag="hs")
+            hst = codes.tile([P, D], BF16, name="hst", tag="ct", align_bytes=64)
             nc.sync.dma_start(out=hst[:], in_=hs_view[:, h, :])
             hs.append(hst)
         load_scales(embp, embeddings_scales, 0, P)
+        for g in range(PASSES):
+            for r in range(4):
+                nc.sync.dma_start(
+                    out=kplanes[g][r:P:32, :].bitcast(I32),
+                    in_=Wk_scales[g, r:16:4, :].bitcast(I32),
+                )
+        load_scales(vplane, Wv_scales, 0, D)
 
         def load_unit(u):
-            plane = planes[u % N_PLANES]
             if u < H:
-                load_scales(plane, Wk_scales, u * D, D)
                 return [[load_codes(Wk_words, g, u * D, D) for g in range(PASSES)]]
-            load_scales(plane, Wv_scales, 0, D)
             return [[load_codes(Wv_words, g, half * HALF, HALF) for g in range(PASSES)] for half in range(2)]
 
         loaded = {0: load_unit(0)}
@@ -182,6 +188,13 @@ def tile_engramgating_kernel(
             cs = slice(j * NT, (j + 1) * NT)
             pb = spread(ident[:, 96 + j : 97 + j])
             nc.scalar.copy(out=bvb[:, cs], in_=pb[:])
+        for h in range(H):
+            for j in range(CH):
+                cs = slice(j * NT, (j + 1) * NT)
+                js = work.tile([P, NT], BF16, name="js", tag="js")
+                nc.scalar.activation(
+                    out=js[:], in_=hs[h][:, cs], func=FN.Square, accum_out=st5[:, 1, h, j : j + 1]
+                )
 
         def chain1(a, b):
             nc.vector.tensor_reduce(out=st[:, :, a:b], in_=st5[:, :, a:b, :], axis=AX.X, op=ALU.add)
@@ -210,20 +223,13 @@ def tile_engramgating_kernel(
         for u in range(H):
             loaded[u + 1] = load_unit(u + 1)
             cts = loaded[u][0]
-            plane = planes[u % N_PLANES]
-            for j in range(CH):
-                cs = slice(j * NT, (j + 1) * NT)
-                js = work.tile([P, NT], BF16, name="js", tag="js")
-                nc.scalar.activation(
-                    out=js[:], in_=hs[u][:, cs], func=FN.Square, accum_out=st5[:, 1, u, j : j + 1]
-                )
             accs = []
             for j in range(CH):
                 acc = ps.tile([P, NT], F32, name="acc", tag="ps")
                 accs.append(acc)
             for g in range(PASSES):
                 for j in range(CH):
-                    mx(accs[j], g, cts[g], j * NT, plane, j * NT, NT)
+                    mx(accs[j], g, cts[g], j * NT, kplanes[g][:, u * D + j * NT : u * D + (j + 1) * NT], NT)
             kbs = []
             for j in range(CH):
                 cs = slice(j * NT, (j + 1) * NT)
@@ -250,7 +256,6 @@ def tile_engramgating_kernel(
                 chain3(0, H - 1)
 
         chain1(H - 1, H)
-        plane = planes[H % N_PLANES]
         outs = []
         for h in range(H):
             ot = big.tile([P, D], F32, name="ot", tag="w")
@@ -265,7 +270,7 @@ def tile_engramgating_kernel(
                 accs.append(acc)
             for g in range(PASSES):
                 for i, (off, n) in enumerate(HALF_GROUPS):
-                    mx(accs[i], g, cts[g], off, plane, c0 + off, n)
+                    mx(accs[i], g, cts[g], off, vplane[:, g, c0 + off : c0 + off + n], n)
             for i, (off, n) in enumerate(HALF_GROUPS):
                 cs = slice(c0 + off, c0 + off + n)
                 nc.vector.tensor_tensor(out=vb[:, cs], in0=accs[i][:, 0:n], in1=bvb[:, cs], op=ALU.add)

@@ -58,14 +58,14 @@ def tile_engramgating_kernel(
         g2t = keep.tile([64, NT], BF16, name="g2t")
         gprod = keep.tile([64, NT], F32, name="gprod")
         ghi = keep.tile([64, NT], BF16, name="ghi")
-        rows = keep.tile([P, NT], BF16, name="rows")
+        rowsg = keep.tile([P, NT], BF16, name="rowsg")
+        rowsb = keep.tile([P, NT], BF16, name="rowsb")
         embc = keep.tile([P, PASSES, 2 * P], U8, name="embc", align_bytes=64)
         embp = keep.tile([P, PASSES, P], U8, name="embp", align_bytes=64)
-        kplanes = []
-        for g in range(PASSES):
-            pl = keep.tile([P, H * D], U8, name="kplane%d" % g, align_bytes=64)
-            kplanes.append(pl)
-        vplane = keep.tile([P, PASSES, D], U8, name="vplane", align_bytes=64)
+        planes = []
+        for u in range(H + 1):
+            pl = keep.tile([P, PASSES, D], U8, name="plane%d" % u, align_bytes=64)
+            planes.append(pl)
         bvb = keep.tile([P, D], BF16, name="bvb")
         vb = keep.tile([P, D], F32, name="vb")
         st5 = keep.tile([P, 3, H, CH], F32, name="st5")
@@ -84,11 +84,11 @@ def tile_engramgating_kernel(
         one = keep.tile([P, 1], F32, name="one")
         warm = keep.tile([P, 1], F32, name="warm")
 
-        def load_scales(plane, scales_dram, c0, width):
+        def load_scales(queue, view, plane, scales_dram, c0, width):
             for r in range(4):
-                nc.sync.dma_start(
-                    out=plane[r:P:32, :, 0:width].bitcast(I32),
-                    in_=scales_dram[:, r:16:4, c0 : c0 + width].rearrange("g q n -> q g n").bitcast(I32),
+                queue.dma_start(
+                    out=plane[r:P:32, :, 0:width].bitcast(view),
+                    in_=scales_dram[:, r:16:4, c0 : c0 + width].rearrange("g q n -> q g n").bitcast(view),
                 )
 
         def load_codes(words_dram, g, c0, width):
@@ -110,28 +110,26 @@ def tile_engramgating_kernel(
                 stop=(g == PASSES - 1),
             )
 
+        nc.vector.memset(rowsb[:], 0.0)
         nc.vector.memset(g1t[:], 0.0)
         nc.vector.memset(g2t[:], 0.0)
-        nc.vector.memset(rows[:], 0.0)
+        nc.vector.memset(rowsg[:], 0.0)
         nc.vector.memset(one[:], 1.0)
         nc.vector.memset(embp[:].bitcast(I32), 0)
-        nc.vector.memset(kplanes[0][:].bitcast(I32), 0)
-        nc.vector.memset(kplanes[1][:].bitcast(I32), 0)
-        make_identity(nc, ident[:])
-        for g in range(2, PASSES):
-            nc.gpsimd.memset(kplanes[g][:].bitcast(F32), 0.0)
-        nc.gpsimd.memset(vplane[:].bitcast(F32), 0.0)
+        nc.vector.memset(planes[0][:].bitcast(I32), 0)
+        nc.vector.memset(planes[1][:].bitcast(I32), 0)
 
         g1v = g1.rearrange("h (c n) -> (h c) n", n=NT)
         g2v = g2.rearrange("h (c n) -> (h c) n", n=NT)
         bkv = bk.rearrange("h (c n) -> (h c) n", n=NT)
         bvv = bv.rearrange("(c n) -> c n", n=NT)
+        nc.gpsimd.dma_start(out=rowsb[0 : H * CH, :], in_=bkv)
+        nc.gpsimd.dma_start(out=rowsb[32 : 32 + CH, :], in_=bvv)
+        make_identity(nc, ident[:])
         nc.scalar.dma_start(out=g1t[0 : H * CH, :], in_=g1v)
         nc.scalar.dma_start(out=g2t[0 : H * CH, :], in_=g2v)
         nc.scalar.dma_start(out=g1t[32 : 32 + H * CH, :], in_=g1v)
         nc.scalar.dma_start(out=g2t[32 : 32 + H * CH, :], in_=g2v)
-        nc.scalar.dma_start(out=rows[64 : 64 + H * CH, :], in_=bkv)
-        nc.scalar.dma_start(out=rows[96 : 96 + CH, :], in_=bvv)
         nc.scalar.activation(out=warm[:], in_=one[:], func=FN.Sqrt)
 
         nc.sync.dma_start(
@@ -143,14 +141,15 @@ def tile_engramgating_kernel(
             hst = codes.tile([P, D], BF16, name="hst", tag="ct", align_bytes=64)
             nc.sync.dma_start(out=hst[:], in_=hs_view[:, h, :])
             hs.append(hst)
-        load_scales(embp, embeddings_scales, 0, P)
-        for g in range(PASSES):
-            for r in range(4):
-                nc.sync.dma_start(
-                    out=kplanes[g][r:P:32, :].bitcast(I32),
-                    in_=Wk_scales[g, r:16:4, :].bitcast(I32),
-                )
-        load_scales(vplane, Wv_scales, 0, D)
+            if h == 0:
+                load_scales(nc.sync, I32, embp, embeddings_scales, 0, P)
+        for u in range(H + 1):
+            if u >= 2:
+                nc.gpsimd.memset(planes[u][:].bitcast(F32), 0.0)
+            if u < H:
+                load_scales(nc.gpsimd, F32, planes[u], Wk_scales, u * D, D)
+            else:
+                load_scales(nc.gpsimd, F32, planes[u], Wv_scales, 0, D)
 
         def load_unit(u):
             if u < H:
@@ -161,11 +160,11 @@ def tile_engramgating_kernel(
 
         nc.vector.tensor_tensor(out=gprod[:], in0=g1t[:], in1=g2t[:], op=ALU.mult)
         nc.vector.tensor_tensor(out=selg[:], in0=ident[:, 0:32], in1=ident[:, 32:64], op=ALU.add)
-        nc.vector.tensor_copy(out=rows[0:32, :], in_=gprod[0:32, :])
+        nc.vector.tensor_copy(out=rowsg[0:32, :], in_=gprod[0:32, :])
         nc.vector.tensor_copy(out=ghi[32:64, :], in_=gprod[32:64, :])
-        nc.vector.tensor_tensor(out=rows[32:64, :], in0=gprod[32:64, :], in1=ghi[32:64, :], op=ALU.subtract)
+        nc.vector.tensor_tensor(out=rowsg[32:64, :], in0=gprod[32:64, :], in1=ghi[32:64, :], op=ALU.subtract)
 
-        def spread(sel_col):
+        def spread(sel_col, rows):
             pt = ps.tile([P, NT], F32, name="pt", tag="ps")
             nc.tensor.matmul(out=pt[:], lhsT=sel_col.to_broadcast([P, P]), rhs=rows[:], start=True, stop=True)
             return pt
@@ -177,17 +176,25 @@ def tile_engramgating_kernel(
             bkb = big.tile([P, D], BF16, name="bkb", tag="bkb")
             wts.append(wt)
             bkbs.append(bkb)
+
+        def spread_bias(h, j):
+            cs = slice(j * NT, (j + 1) * NT)
+            if h < H:
+                pb = spread(ident[:, h * CH + j : h * CH + j + 1], rowsb)
+                nc.scalar.copy(out=bkbs[h][:, cs], in_=pb[:])
+            else:
+                pb = spread(ident[:, 32 + j : 33 + j], rowsb)
+                nc.scalar.copy(out=bvb[:, cs], in_=pb[:])
+
+        for j in range(CH):
+            spread_bias(0, j)
+        for h in range(H):
             for j in range(CH):
                 c = h * CH + j
                 cs = slice(j * NT, (j + 1) * NT)
-                pg = spread(selg[:, c : c + 1])
-                pb = spread(ident[:, 64 + c : 65 + c])
-                nc.vector.tensor_tensor(out=wt[:, cs], in0=pg[:], in1=hs[h][:, cs], op=ALU.mult)
-                nc.scalar.copy(out=bkb[:, cs], in_=pb[:])
-        for j in range(CH):
-            cs = slice(j * NT, (j + 1) * NT)
-            pb = spread(ident[:, 96 + j : 97 + j])
-            nc.scalar.copy(out=bvb[:, cs], in_=pb[:])
+                pg = spread(selg[:, c : c + 1], rowsg)
+                nc.vector.tensor_tensor(out=wts[h][:, cs], in0=pg[:], in1=hs[h][:, cs], op=ALU.mult)
+                spread_bias(h + 1, j)
         for h in range(H):
             for j in range(CH):
                 cs = slice(j * NT, (j + 1) * NT)
@@ -229,7 +236,7 @@ def tile_engramgating_kernel(
                 accs.append(acc)
             for g in range(PASSES):
                 for j in range(CH):
-                    mx(accs[j], g, cts[g], j * NT, kplanes[g][:, u * D + j * NT : u * D + (j + 1) * NT], NT)
+                    mx(accs[j], g, cts[g], j * NT, planes[u][:, g, j * NT : (j + 1) * NT], NT)
             kbs = []
             for j in range(CH):
                 cs = slice(j * NT, (j + 1) * NT)
@@ -270,7 +277,7 @@ def tile_engramgating_kernel(
                 accs.append(acc)
             for g in range(PASSES):
                 for i, (off, n) in enumerate(HALF_GROUPS):
-                    mx(accs[i], g, cts[g], off, vplane[:, g, c0 + off : c0 + off + n], n)
+                    mx(accs[i], g, cts[g], off, planes[H][:, g, c0 + off : c0 + off + n], n)
             for i, (off, n) in enumerate(HALF_GROUPS):
                 cs = slice(c0 + off, c0 + off + n)
                 nc.vector.tensor_tensor(out=vb[:, cs], in0=accs[i][:, 0:n], in1=bvb[:, cs], op=ALU.add)

@@ -23,6 +23,8 @@ CH = D // NT
 EPS = 2.0 ** -23
 HALF = D // 2
 HALF_GROUPS = ((0, 512), (512, 512), (1024, 256))
+QUADRANT_ORDER = (0, 2, 1, 3)
+VECTOR_ZEROES = 3
 
 
 def tile_engramgating_kernel(
@@ -62,10 +64,8 @@ def tile_engramgating_kernel(
         rowsb = keep.tile([P, NT], BF16, name="rowsb")
         embc = keep.tile([P, PASSES, 2 * P], U8, name="embc", align_bytes=64)
         embp = keep.tile([P, PASSES, P], U8, name="embp", align_bytes=64)
-        planes = []
-        for u in range(H + 1):
-            pl = keep.tile([P, PASSES, D], U8, name="plane%d" % u, align_bytes=64)
-            planes.append(pl)
+        kplane = keep.tile([P, PASSES, H * D], U8, name="kplane", align_bytes=64)
+        vplane = keep.tile([P, PASSES, D], U8, name="vplane", align_bytes=64)
         bvb = keep.tile([P, D], BF16, name="bvb")
         vb = keep.tile([P, D], F32, name="vb")
         st5 = keep.tile([P, 3, H, CH], F32, name="st5")
@@ -84,11 +84,11 @@ def tile_engramgating_kernel(
         one = keep.tile([P, 1], F32, name="one")
         warm = keep.tile([P, 1], F32, name="warm")
 
-        def load_scales(queue, view, plane, scales_dram, c0, width):
-            for r in range(4):
-                queue.dma_start(
-                    out=plane[r:P:32, :, 0:width].bitcast(view),
-                    in_=scales_dram[:, r:16:4, c0 : c0 + width].rearrange("g q n -> q g n").bitcast(view),
+        def load_scales(plane, scales_dram):
+            for q in QUADRANT_ORDER:
+                nc.sync.dma_start(
+                    out=plane[32 * q : 32 * q + 4, :, :].bitcast(I32),
+                    in_=scales_dram[:, 4 * q : 4 * q + 4, :].rearrange("g r n -> r g n").bitcast(I32),
                 )
 
         def load_codes(words_dram, g, c0, width):
@@ -116,8 +116,7 @@ def tile_engramgating_kernel(
         nc.vector.memset(rowsg[:], 0.0)
         nc.vector.memset(one[:], 1.0)
         nc.vector.memset(embp[:].bitcast(I32), 0)
-        nc.vector.memset(planes[0][:].bitcast(I32), 0)
-        nc.vector.memset(planes[1][:].bitcast(I32), 0)
+        nc.vector.memset(kplane[:, 0:VECTOR_ZEROES, :].bitcast(I32), 0)
 
         g1v = g1.rearrange("h (c n) -> (h c) n", n=NT)
         g2v = g2.rearrange("h (c n) -> (h c) n", n=NT)
@@ -126,6 +125,8 @@ def tile_engramgating_kernel(
         nc.gpsimd.dma_start(out=rowsb[0 : H * CH, :], in_=bkv)
         nc.gpsimd.dma_start(out=rowsb[32 : 32 + CH, :], in_=bvv)
         make_identity(nc, ident[:])
+        nc.gpsimd.memset(kplane[:, VECTOR_ZEROES:PASSES, :].bitcast(F32), 0.0)
+        nc.gpsimd.memset(vplane[:].bitcast(F32), 0.0)
         nc.scalar.dma_start(out=g1t[0 : H * CH, :], in_=g1v)
         nc.scalar.dma_start(out=g2t[0 : H * CH, :], in_=g2v)
         nc.scalar.dma_start(out=g1t[32 : 32 + H * CH, :], in_=g1v)
@@ -141,15 +142,9 @@ def tile_engramgating_kernel(
             hst = codes.tile([P, D], BF16, name="hst", tag="ct", align_bytes=64)
             nc.sync.dma_start(out=hst[:], in_=hs_view[:, h, :])
             hs.append(hst)
-            if h == 0:
-                load_scales(nc.sync, I32, embp, embeddings_scales, 0, P)
-        for u in range(H + 1):
-            if u >= 2:
-                nc.gpsimd.memset(planes[u][:].bitcast(F32), 0.0)
-            if u < H:
-                load_scales(nc.gpsimd, F32, planes[u], Wk_scales, u * D, D)
-            else:
-                load_scales(nc.gpsimd, F32, planes[u], Wv_scales, 0, D)
+        load_scales(embp, embeddings_scales)
+        load_scales(kplane, Wk_scales)
+        load_scales(vplane, Wv_scales)
 
         def load_unit(u):
             if u < H:
@@ -236,7 +231,7 @@ def tile_engramgating_kernel(
                 accs.append(acc)
             for g in range(PASSES):
                 for j in range(CH):
-                    mx(accs[j], g, cts[g], j * NT, planes[u][:, g, j * NT : (j + 1) * NT], NT)
+                    mx(accs[j], g, cts[g], j * NT, kplane[:, g, u * D + j * NT : u * D + (j + 1) * NT], NT)
             kbs = []
             for j in range(CH):
                 cs = slice(j * NT, (j + 1) * NT)
@@ -277,7 +272,7 @@ def tile_engramgating_kernel(
                 accs.append(acc)
             for g in range(PASSES):
                 for i, (off, n) in enumerate(HALF_GROUPS):
-                    mx(accs[i], g, cts[g], off, planes[H][:, g, c0 + off : c0 + off + n], n)
+                    mx(accs[i], g, cts[g], off, vplane[:, g, c0 + off : c0 + off + n], n)
             for i, (off, n) in enumerate(HALF_GROUPS):
                 cs = slice(c0 + off, c0 + off + n)
                 nc.vector.tensor_tensor(out=vb[:, cs], in0=accs[i][:, 0:n], in1=bvb[:, cs], op=ALU.add)

from contextlib import ExitStack

import concourse.mybir as mybir
from concourse.masks import make_identity

FLOPS = 2 * 128 * 2560 * 12800

F32 = mybir.dt.float32
BF16 = mybir.dt.bfloat16
U8 = mybir.dt.uint8
I32 = mybir.dt.int32
FP4X4 = mybir.dt.float4_e2m1fn_x4
ALU = mybir.AluOpType
FN = mybir.ActivationFunctionType
AX = mybir.AxisListType

P = 128
D = 2560
H = 4
PASSES = 5
NT = 512
CH = D // NT
EPS = 2.0 ** -23
HALF = D // 2
HALF_GROUPS = ((0, 512), (512, 512), (1024, 256))
QUADRANT_ORDER = (0, 2, 1, 3)
VECTOR_ZEROES = 3


def tile_engramgating_kernel(
    tc,
    embeddings_words,
    embeddings_scales,
    hidden_states,
    Wv_words,
    Wv_scales,
    bv,
    Wk_words,
    Wk_scales,
    bk,
    g1,
    g2,
    out,
):
    nc = tc.nc
    hs_view = hidden_states.rearrange("b s h d -> (b s) h d")
    out_view = out.rearrange("b s h d -> (b s) h d")

    with ExitStack() as ctx:
        keep = ctx.enter_context(tc.tile_pool(name="keep", bufs=1))
        codes = ctx.enter_context(tc.tile_pool(name="codes", bufs=12))
        big = ctx.enter_context(tc.tile_pool(name="big", bufs=4))
        work = ctx.enter_context(tc.tile_pool(name="work", bufs=2))
        ps = ctx.enter_context(tc.psum_pool(name="ps", bufs=8))
        ctx.enter_context(tc.manual_schedule())

        ident = keep.tile([P, P], BF16, name="ident")
        selg = keep.tile([P, 32], BF16, name="selg")
        g1t = keep.tile([64, NT], BF16, name="g1t")
        g2t = keep.tile([64, NT], BF16, name="g2t")
        gprod = keep.tile([64, NT], F32, name="gprod")
        ghi = keep.tile([64, NT], BF16, name="ghi")
        rowsg = keep.tile([P, NT], BF16, name="rowsg")
        rowsb = keep.tile([P, NT], BF16, name="rowsb")
        embc = keep.tile([P, PASSES, 2 * P], U8, name="embc", align_bytes=64)
        embp = keep.tile([P, PASSES, P], U8, name="embp", align_bytes=64)
        kplane = keep.tile([P, PASSES, H * D], U8, name="kplane", align_bytes=64)
        vplane = keep.tile([P, PASSES, D], U8, name="vplane", align_bytes=64)
        bvb = keep.tile([P, D], BF16, name="bvb")
        vb = keep.tile([P, D], F32, name="vb")
        st5 = keep.tile([P, 3, H, CH], F32, name="st5")
        st = keep.tile([P, 3, H], F32, name="st")
        msq = keep.tile([P, 2, H], F32, name="msq")
        rms = keep.tile([P, 2, H], F32, name="rms")
        den = keep.tile([P, H], F32, name="den")
        rden = keep.tile([P, H], F32, name="rden")
        aval = keep.tile([P, H], F32, name="aval")
        aabs = keep.tile([P, H], F32, name="aabs")
        aclip = keep.tile([P, H], F32, name="aclip")
        aroot = keep.tile([P, H], F32, name="aroot")
        asign = keep.tile([P, H], F32, name="asign")
        cval = keep.tile([P, H], F32, name="cval")
        gate = keep.tile([P, H], F32, name="gate")
        one = keep.tile([P, 1], F32, name="one")
        warm = keep.tile([P, 1], F32, name="warm")

        def load_scales(plane, scales_dram):
            for q in QUADRANT_ORDER:
                nc.sync.dma_start(
                    out=plane[32 * q : 32 * q + 4, :, :].bitcast(I32),
                    in_=scales_dram[:, 4 * q : 4 * q + 4, :].rearrange("g r n -> r g n").bitcast(I32),
                )

        def load_codes(words_dram, g, c0, width):
            ct = codes.tile([P, 2 * width], U8, name="ct", tag="ct", align_bytes=64)
            nc.sync.dma_start(
                out=ct[:].bitcast(I32),
                in_=words_dram[g, :, 2 * c0 : 2 * (c0 + width)].bitcast(I32),
            )
            return ct

        def mx(acc, g, ct, off, scale_cols, n):
            nc.tensor.matmul_mx(
                out=acc[:, 0:n],
                lhsT=embc[:, g, :].bitcast(FP4X4),
                lhsT_scale=embp[:, g, :],
                rhs=ct[:, 2 * off : 2 * (off + n)].bitcast(FP4X4),
                rhs_scale=scale_cols,
                start=(g == 0),
                stop=(g == PASSES - 1),
            )

        nc.vector.memset(rowsb[:], 0.0)
        nc.vector.memset(g1t[:], 0.0)
        nc.vector.memset(g2t[:], 0.0)
        nc.vector.memset(rowsg[:], 0.0)
        nc.vector.memset(one[:], 1.0)
        nc.vector.memset(embp[:].bitcast(I32), 0)
        nc.vector.memset(kplane[:, 0:VECTOR_ZEROES, :].bitcast(I32), 0)

        g1v = g1.rearrange("h (c n) -> (h c) n", n=NT)
        g2v = g2.rearrange("h (c n) -> (h c) n", n=NT)
        bkv = bk.rearrange("h (c n) -> (h c) n", n=NT)
        bvv = bv.rearrange("(c n) -> c n", n=NT)
        nc.gpsimd.dma_start(out=rowsb[0 : H * CH, :], in_=bkv)
        nc.gpsimd.dma_start(out=rowsb[32 : 32 + CH, :], in_=bvv)
        make_identity(nc, ident[:])
        nc.gpsimd.memset(kplane[:, VECTOR_ZEROES:PASSES, :].bitcast(F32), 0.0)
        nc.gpsimd.memset(vplane[:].bitcast(F32), 0.0)
        nc.scalar.dma_start(out=g1t[0 : H * CH, :], in_=g1v)
        nc.scalar.dma_start(out=g2t[0 : H * CH, :], in_=g2v)
        nc.scalar.dma_start(out=g1t[32 : 32 + H * CH, :], in_=g1v)
        nc.scalar.dma_start(out=g2t[32 : 32 + H * CH, :], in_=g2v)
        nc.scalar.activation(out=warm[:], in_=one[:], func=FN.Sqrt)

        nc.sync.dma_start(
            out=embc[:].bitcast(I32),
            in_=embeddings_words.rearrange("g p n -> p g n").bitcast(I32),
        )
        hs = []
        for h in range(H):
            hst = codes.tile([P, D], BF16, name="hst", tag="ct", align_bytes=64)
            nc.sync.dma_start(out=hst[:], in_=hs_view[:, h, :])
            hs.append(hst)
        load_scales(embp, embeddings_scales)
        load_scales(kplane, Wk_scales)
        load_scales(vplane, Wv_scales)

        def load_unit(u):
            if u < H:
                return [[load_codes(Wk_words, g, u * D, D) for g in range(PASSES)]]
            return [[load_codes(Wv_words, g, half * HALF, HALF) for g in range(PASSES)] for half in range(2)]

        loaded = {0: load_unit(0)}

        nc.vector.tensor_tensor(out=gprod[:], in0=g1t[:], in1=g2t[:], op=ALU.mult)
        nc.vector.tensor_tensor(out=selg[:], in0=ident[:, 0:32], in1=ident[:, 32:64], op=ALU.add)
        nc.vector.tensor_copy(out=rowsg[0:32, :], in_=gprod[0:32, :])
        nc.vector.tensor_copy(out=ghi[32:64, :], in_=gprod[32:64, :])
        nc.vector.tensor_tensor(out=rowsg[32:64, :], in0=gprod[32:64, :], in1=ghi[32:64, :], op=ALU.subtract)

        def spread(sel_col, rows):
            pt = ps.tile([P, NT], F32, name="pt", tag="ps")
            nc.tensor.matmul(out=pt[:], lhsT=sel_col.to_broadcast([P, P]), rhs=rows[:], start=True, stop=True)
            return pt

        wts = []
        bkbs = []
        for h in range(H):
            wt = big.tile([P, D], F32, name="wt", tag="w")
            bkb = big.tile([P, D], BF16, name="bkb", tag="bkb")
            wts.append(wt)
            bkbs.append(bkb)

        def spread_bias(h, j):
            cs = slice(j * NT, (j + 1) * NT)
            if h < H:
                pb = spread(ident[:, h * CH + j : h * CH + j + 1], rowsb)
                nc.scalar.copy(out=bkbs[h][:, cs], in_=pb[:])
            else:
                pb = spread(ident[:, 32 + j : 33 + j], rowsb)
                nc.scalar.copy(out=bvb[:, cs], in_=pb[:])

        for j in range(CH):
            spread_bias(0, j)
        for h in range(H):
            for j in range(CH):
                c = h * CH + j
                cs = slice(j * NT, (j + 1) * NT)
                pg = spread(selg[:, c : c + 1], rowsg)
                nc.vector.tensor_tensor(out=wts[h][:, cs], in0=pg[:], in1=hs[h][:, cs], op=ALU.mult)
                spread_bias(h + 1, j)
        for h in range(H):
            for j in range(CH):
                cs = slice(j * NT, (j + 1) * NT)
                js = work.tile([P, NT], BF16, name="js", tag="js")
                nc.scalar.activation(
                    out=js[:], in_=hs[h][:, cs], func=FN.Square, accum_out=st5[:, 1, h, j : j + 1]
                )

        def chain1(a, b):
            nc.vector.tensor_reduce(out=st[:, :, a:b], in_=st5[:, :, a:b, :], axis=AX.X, op=ALU.add)
            nc.vector.tensor_scalar(
                out=msq[:, :, a:b], in0=st[:, 0:2, a:b], scalar1=1.0 / D, scalar2=EPS, op0=ALU.mult, op1=ALU.add
            )
            nc.scalar.activation(out=rms[:, :, a:b], in_=msq[:, :, a:b], func=FN.Sqrt)

        def chain2(a, b):
            nc.vector.tensor_tensor(out=den[:, a:b], in0=rms[:, 0, a:b], in1=rms[:, 1, a:b], op=ALU.mult)
            nc.vector.reciprocal(out=rden[:, a:b], in_=den[:, a:b])
            nc.vector.scalar_tensor_tensor(
                out=aval[:, a:b], in0=st[:, 2, a:b], scalar=D ** -0.5, in1=rden[:, a:b], op0=ALU.mult, op1=ALU.mult
            )
            nc.vector.scalar_tensor_tensor(
                out=aabs[:, a:b], in0=aval[:, a:b], scalar=-1.0, in1=aval[:, a:b], op0=ALU.mult, op1=ALU.max
            )
            nc.vector.tensor_scalar_max(out=aclip[:, a:b], in0=aabs[:, a:b], scalar1=1e-6)
            nc.scalar.activation(out=aroot[:, a:b], in_=aclip[:, a:b], func=FN.Sqrt)
            nc.scalar.activation(out=asign[:, a:b], in_=aval[:, a:b], func=FN.Sign)

        def chain3(a, b):
            nc.vector.tensor_tensor(out=cval[:, a:b], in0=aroot[:, a:b], in1=asign[:, a:b], op=ALU.mult)
            nc.scalar.activation(out=gate[:, a:b], in_=cval[:, a:b], func=FN.Sigmoid)

        for u in range(H):
            loaded[u + 1] = load_unit(u + 1)
            cts = loaded[u][0]
            accs = []
            for j in range(CH):
                acc = ps.tile([P, NT], F32, name="acc", tag="ps")
                accs.append(acc)
            for g in range(PASSES):
                for j in range(CH):
                    mx(accs[j], g, cts[g], j * NT, kplane[:, g, u * D + j * NT : u * D + (j + 1) * NT], NT)
            kbs = []
            for j in range(CH):
                cs = slice(j * NT, (j + 1) * NT)
                kb = work.tile([P, NT], F32, name="kb", tag="kb", bufs=6)
                kbs.append(kb)
                nc.vector.tensor_tensor(out=kb[:], in0=accs[j][:], in1=bkbs[u][:, cs], op=ALU.add)
                js = work.tile([P, NT], BF16, name="js", tag="js")
                nc.scalar.activation(out=js[:], in_=kb[:], func=FN.Square, accum_out=st5[:, 0, u, j : j + 1])
            for j in range(CH):
                cs = slice(j * NT, (j + 1) * NT)
                jv = work.tile([P, NT], F32, name="jv", tag="jv")
                nc.vector.scalar_tensor_tensor(
                    out=jv[:],
                    in0=kbs[j][:],
                    scalar=1.0,
                    in1=wts[u][:, cs],
                    op0=ALU.mult,
                    op1=ALU.mult,
                    accum_out=st5[:, 2, u, j : j + 1],
                )
            if u == H - 2:
                chain1(0, H - 1)
                chain2(0, H - 1)
                chain3(0, H - 1)

        chain1(H - 1, H)
        outs = []
        for h in range(H):
            ot = big.tile([P, D], F32, name="ot", tag="w")
            outs.append(ot)
        for half in range(2):
            cts = loaded[H][half]
            c0 = half * HALF
            hcs = slice(c0, c0 + HALF)
            accs = []
            for i in range(len(HALF_GROUPS)):
                acc = ps.tile([P, NT], F32, name="acc", tag="ps")
                accs.append(acc)
            for g in range(PASSES):
                for i, (off, n) in enumerate(HALF_GROUPS):
                    mx(accs[i], g, cts[g], off, vplane[:, g, c0 + off : c0 + off + n], n)
            for i, (off, n) in enumerate(HALF_GROUPS):
                cs = slice(c0 + off, c0 + off + n)
                nc.vector.tensor_tensor(out=vb[:, cs], in0=accs[i][:, 0:n], in1=bvb[:, cs], op=ALU.add)
            nc.vector.tensor_scalar_mul(out=outs[0][:, hcs], in0=vb[:, hcs], scalar1=gate[:, 0:1])
            nc.scalar.activation(out=outs[1][:, hcs], in_=vb[:, hcs], func=FN.Copy, scale=gate[:, 1:2])
            nc.vector.tensor_scalar_mul(out=outs[2][:, hcs], in0=vb[:, hcs], scalar1=gate[:, 2:3])
            for h in range(H - 1):
                nc.sync.dma_start(out=out_view[:, h, hcs], in_=outs[h][:, hcs])
            if half == 0:
                chain2(H - 1, H)
            else:
                chain3(H - 1, H)
        last = H - 1
        nc.vector.tensor_scalar_mul(out=outs[last][:, 0:HALF], in0=vb[:, 0:HALF], scalar1=gate[:, last : last + 1])
        nc.scalar.activation(
            out=outs[last][:, HALF:D], in_=vb[:, HALF:D], func=FN.Copy, scale=gate[:, last : last + 1]
        )
        nc.sync.dma_start(out=out_view[:, last, 0:HALF], in_=outs[last][:, 0:HALF])
        nc.sync.dma_start(out=out_view[:, last, HALF:D], in_=outs[last][:, HALF:D])
